import numpy as np
import ml_dtypes


def mxq(x, axis, fmt="e4m3"):
    dtype, down = {"e4m3": (ml_dtypes.float8_e4m3fn, 7), "e5m2": (ml_dtypes.float8_e5m2, 14)}[fmt]
    v = np.moveaxis(np.asarray(x, np.float32).astype(ml_dtypes.bfloat16).astype(np.float64), axis, -1)
    blocks = v.reshape(v.shape[:-1] + (-1, 32))
    amax = np.abs(blocks).max(-1, keepdims=True)
    byte = np.maximum(np.where(amax > 0, np.frexp(amax)[1] - 1 + 127, 0) - down, 1)
    scale = np.exp2(byte - 127.0)
    codes = (blocks / scale).astype(np.float32).astype(dtype).astype(np.float64)
    return np.moveaxis((codes * scale).reshape(v.shape), -1, axis)


WIDE = False


def mx_kscale(k):
    if not WIDE:
        return np.ones(k)
    levels = np.array([10, -10, 5, -5, 0])
    if k % 512:
        return np.exp2(np.random.permutation(np.resize(levels, k // 32))).repeat(32)
    a = np.empty((k // 512, 16))
    for p in range(k // 512):
        a[p, :8] = np.random.permutation(np.resize(levels, 8))
        for g in range(8):
            far = levels[np.abs(levels - a[p, g]) >= 10]
            a[p, g + 8] = far[np.random.randint(len(far))]
    return np.exp2(a.ravel()).repeat(32)


BF16 = ml_dtypes.bfloat16


def bf(x):
    return np.asarray(x, np.float32).astype(BF16)


def f64(x):
    return np.asarray(x).astype(np.float64)


B, S, DV, D, H, A = 2, 256, 1024, 1024, 8, 64
LN_EPS = 1e-3


def setup_inputs():
    s = mx_kscale(DV)
    return {
        "attn": bf(np.random.standard_normal((B, H, S, DV)) * 0.4 * s),
        "Wo": bf(np.random.standard_normal((H, DV, D)) * 0.6 / np.sqrt(DV * H) / s[None, :, None]),
        "bo": bf(np.random.standard_normal((H, D)) * 0.12 / np.sqrt(H)),
        "query_inputs": bf(np.random.standard_normal((B, S, D)) * 0.1),
        "gamma": bf(1.0 + 0.1 * np.random.standard_normal(D)),
        "beta": bf(0.1 * np.random.standard_normal(D)),
    }


def reference(attn, Wo, bo, query_inputs, gamma, beta):
    pre = mxq(f64(attn), 3, "e4m3") @ mxq(f64(Wo), 1, "e4m3")
    head_out = np.maximum(pre + f64(bo)[None, :, None, :], 0.0)
    x = f64(query_inputs) + head_out.sum(axis=1)
    mean = x.mean(axis=-1, keepdims=True)
    var = x.var(axis=-1, keepdims=True)
    return f64(gamma) * (x - mean) / np.sqrt(var + LN_EPS) + f64(beta)

@@ -1,0 +1,338 @@
+from contextlib import ExitStack
+
+import concourse.mybir as mybir
+from concourse.masks import make_identity
+
+F32 = mybir.dt.float32
+BF16 = mybir.dt.bfloat16
+U32 = mybir.dt.uint32
+U8 = mybir.dt.uint8
+FP8X4 = mybir.dt.float8_e4m3fn_x4
+ALU = mybir.AluOpType
+ACT = mybir.ActivationFunctionType
+
+P = 128
+B, H, S, DV, D = 2, 8, 256, 1024, 1024
+NS = B * S
+G = DV // 512
+DT = D // P
+HALF = D // 2
+UNITS = 2 * H
+LN_EPS = 1e-3
+FLOPS = 2 * B * H * S * DV * D
+
+S_HEADS = (0, 2, 4, 7)
+MAIN = 384
+
+
+def tile_multiheadattentionunit_pa_kernel(tc, attn, Wo, bo, query_inputs, gamma, beta, out):
+    nc = tc.nc
+    with ExitStack() as ctx:
+        const = ctx.enter_context(tc.tile_pool(name="const", bufs=1))
+        wraw_pool = ctx.enter_context(tc.tile_pool(name="wraw", bufs=3))
+        wgrp_pool = ctx.enter_context(tc.tile_pool(name="wgrp", bufs=3))
+        wlast_pool = ctx.enter_context(tc.tile_pool(name="wlast", bufs=1))
+        wq_pool = ctx.enter_context(tc.tile_pool(name="wq", bufs=4))
+        araw_pool = ctx.enter_context(tc.tile_pool(name="araw", bufs=3))
+        agrp_pool = ctx.enter_context(tc.tile_pool(name="agrp", bufs=3))
+        aq_pool = ctx.enter_context(tc.tile_pool(name="aq", bufs=3))
+        small = ctx.enter_context(tc.tile_pool(name="small", bufs=4))
+        ps_xt = ctx.enter_context(tc.psum_pool(name="ps_xt", bufs=2))
+        ps_mm = ctx.enter_context(tc.psum_pool(name="ps_mm", bufs=6))
+        ctx.enter_context(tc.manual_schedule())
+
+        a_raws = {}
+        w_raws = {}
+
+        def load_a(h, src):
+            a_raw = araw_pool.tile([P, 4, DV], BF16, name="a_raw")
+            nc.sync.dma_start(
+                out=a_raw[:].rearrange("p (b t) k -> p b (t k)", b=B),
+                in_=src.rearrange("b (p t) k -> p b (t k)", t=2),
+            )
+            a_raws[h] = a_raw
+
+        def load_w(h):
+            w_raw = wraw_pool.tile([P, 8 * D], BF16, name="w_raw")
+            w_raws[h] = w_raw
+            if h == 0:
+                rows = w_raw[:].rearrange("p (a e d) -> p a e d", a=2, e=4)
+                for dh in range(2):
+                    for a in range(2):
+                        nc.sync.dma_start(
+                            out=rows[:, a, :, dh * HALF : (dh + 1) * HALF],
+                            in_=Wo[h, a * 512 : (a + 1) * 512, dh * HALF : (dh + 1) * HALF].rearrange(
+                                "(p e) d -> p e d", e=4
+                            ),
+                        )
+            else:
+                nc.sync.dma_start(
+                    out=w_raw[:].rearrange("p (a x) -> p a x", a=2),
+                    in_=Wo[h].rearrange("(a p e) d -> p a (e d)", a=2, e=4),
+                )
+
+        for h in range(3):
+            load_a(h, attn[:, h])
+            load_w(h)
+
+        warm = const.tile([P, 1], F32, name="warm")
+        nc.vector.memset(warm[:], 1.0)
+        nc.scalar.activation(out=warm[:], in_=warm[:], func=ACT.Sqrt)
+        ident_f = const.tile([P, P], F32, name="ident_f")
+        make_identity(nc, ident_f[:])
+        ident_b = const.tile([P, P], BF16, name="ident_b")
+        make_identity(nc, ident_b[:])
+        ones_b = const.tile([P, P], BF16, name="ones_b")
+        nc.vector.memset(ones_b[:], 1.0)
+        bo_t = const.tile([P, P], BF16, name="bo_t")
+        nc.vector.memset(bo_t[:], 0.0)
+        nc.scalar.dma_start(out=bo_t[0 : H * DT, :], in_=bo.rearrange("h (t c) -> (h t) c", c=P))
+        bo_pad = const.tile([P, D], BF16, name="bo_pad")
+        nc.vector.memset(bo_pad[:], 0.0)
+        v_heads = [h for h in range(H) if h not in S_HEADS]
+        for r, h in enumerate(v_heads):
+            nc.scalar.dma_start(out=bo_pad[r : r + 1, :], in_=bo[h : h + 1, :])
+        gamma_b = const.tile([P, D], BF16, name="gamma_b")
+        beta_b = const.tile([P, D], BF16, name="beta_b")
+
+        bT_ps = ps_xt.tile([P, P], BF16, name="bT_ps", tag="xt")
+        nc.tensor.transpose(bT_ps[:], bo_t[:], ident_b[:])
+        bpos = const.tile([P, P], F32, name="bpos")
+        nc.vector.tensor_copy(out=bpos[:], in_=bT_ps[:])
+        negb = const.tile([P, P], F32, name="negb")
+        nc.vector.tensor_scalar(out=negb[:], in0=bT_ps[:], scalar1=-1.0, scalar2=None, op0=ALU.mult)
+
+        xts = {}
+        a_grps = {}
+        a_q = {}
+        w_grps = {}
+        w_lasts = {}
+        w_q = {}
+        pss = {}
+        accs = []
+
+        def in_range(k):
+            return 0 <= k < UNITS
+
+        def pe_transposes(k):
+            h, g = divmod(k, 2)
+            a_raw = a_raws[h]
+            xts[k] = []
+            for half in range(2):
+                xt = ps_xt.tile([P, 2, 256], F32, name="xt", tag="xt")
+                for jj in range(2):
+                    words = a_raw[:, 2 * half + jj, :].bitcast(F32)
+                    for u in range(2):
+                        nc.tensor.transpose(
+                            xt[:, u, jj * P : (jj + 1) * P], words[:, 256 * g + u : 256 * (g + 1) : 2], ident_f[:]
+                        )
+                xts[k].append(xt)
+
+        def s_exits(k):
+            a_grp = agrp_pool.tile([P, NS * 2], F32, name="a_grp", align_bytes=64)
+            a_grp3 = a_grp[:].rearrange("p (c u) -> p c u", u=2)
+            for half in range(2):
+                nc.scalar.copy(
+                    out=a_grp3[:, half * 256 : (half + 1) * 256, :],
+                    in_=xts[k][half][:].rearrange("p u c -> p c u"),
+                )
+            a_grps[k] = a_grp
+
+        def v_quant_a(k):
+            h, g = divmod(k, 2)
+            if g == 0:
+                a_codes = aq_pool.tile([P, G * NS], U32, name="a_codes", align_bytes=64)
+                a_sc = aq_pool.tile([P, G * NS], U8, name="a_sc", align_bytes=64)
+                a_q[h] = (a_codes, a_sc)
+            a_codes, a_sc = a_q[h]
+            nc.vector.quantize_mx(
+                out=a_codes[:, g * NS : (g + 1) * NS].bitcast(FP8X4),
+                scales=a_sc[:, g * NS : (g + 1) * NS],
+                in_=a_grps[k][:].bitcast(BF16),
+            )
+
+        def v_copy(o, i):
+            nc.vector.tensor_copy(out=o, in_=i)
+
+        def s_copy(o, i):
+            nc.scalar.copy(out=o, in_=i)
+
+        def g_copy(o, i):
+            nc.gpsimd.tensor_scalar(out=o, in0=i, scalar1=1.0, scalar2=0.0, op0=ALU.mult, op1=ALU.add)
+
+        def regroup(n, copy, c0, c1):
+            if c1 <= c0:
+                return
+            h, dh = divmod(n, 2)
+            if c0 < MAIN:
+                if n not in w_grps:
+                    w_grp_new = wgrp_pool.tile([P, G * MAIN * 4], BF16, name="w_grp", tag="w_grp", align_bytes=64)
+                    w_grps[n] = w_grp_new
+                dst = w_grps[n][:].rearrange("p (g d t) -> p g d t", g=G, t=4)[:, :, c0:c1, :]
+            else:
+                w_last_new = wlast_pool.tile([P, G * P * 4], BF16, name="w_last", align_bytes=64)
+                w_lasts[n] = w_last_new
+                dst = w_last_new[:].rearrange("p (g d t) -> p g d t", g=G, t=4)
+            rows = w_raws[h][:].rearrange("p (r d) -> p r d", r=8)
+            for g in range(G):
+                copy(
+                    dst[:, g, :, :].rearrange("p (c i) t -> p c t i", i=4),
+                    rows[:, 4 * g : 4 * g + 4, dh * HALF + c0 : dh * HALF + c1].rearrange("p t (c i) -> p c t i", i=4),
+                )
+
+        def v_quant_w(n):
+            w_codes = wq_pool.tile([P, G * HALF], U32, name="w_codes", align_bytes=64)
+            w_sc = wq_pool.tile([P, G * HALF], U8, name="w_sc", align_bytes=64)
+            for src, e0, e1, word0 in ((w_grps[n], 0, 2048, 0), (w_grps[n], 2048, 3072, 512), (w_lasts[n], 0, 1024, 768)):
+                words = (e1 - e0) // 4
+                nc.vector.quantize_mx(
+                    out=w_codes[:, word0 : word0 + words].bitcast(FP8X4),
+                    scales=w_sc[:, word0 : word0 + words],
+                    in_=src[:, e0:e1],
+                )
+            w_q[n] = (w_codes, w_sc)
+
+        def pe_mm(n):
+            h, dh = divmod(n, 2)
+            a_codes, a_sc = a_q[h]
+            w_codes, w_sc = w_q[n]
+            pss[n] = []
+            for dd in range(4):
+                ps = ps_mm.tile([P, NS], F32, name="ps", tag="mm")
+                for g in range(G):
+                    w0 = g * MAIN + dd * P if dd < 3 else 2 * MAIN + g * P
+                    nc.tensor.matmul_mx(
+                        out=ps[:],
+                        lhsT=w_codes[:, w0 : w0 + P].bitcast(FP8X4),
+                        lhsT_scale=w_sc[:, w0 : w0 + P],
+                        rhs=a_codes[:, g * NS : (g + 1) * NS].bitcast(FP8X4),
+                        rhs_scale=a_sc[:, g * NS : (g + 1) * NS],
+                        start=(g == 0),
+                        stop=(g == G - 1),
+                    )
+                pss[n].append(ps)
+
+        def take_out(n):
+            h, dh = divmod(n, 2)
+            if h in S_HEADS and dh == 0:
+                acc_new = const.tile([P, DT, NS], F32, name="acc%d" % h)
+                accs.append(acc_new)
+            acc = accs[-1]
+            for dd in range(4):
+                dt = dh * 4 + dd
+                col = h * DT + dt
+                if h in S_HEADS:
+                    nc.scalar.activation(
+                        out=acc[:, dt, :], in_=pss[n][dd][:], func=ACT.Relu, bias=bpos[:, col : col + 1], scale=1.0
+                    )
+                else:
+                    nc.vector.scalar_tensor_tensor(
+                        out=acc[:, dt, :],
+                        in0=pss[n][dd][:],
+                        scalar=negb[:, col : col + 1],
+                        in1=acc[:, dt, :],
+                        op0=ALU.max,
+                        op1=ALU.add,
+                    )
+
+        xps = {}
+
+        def pe_back(j, sums):
+            opening = 0 in sums
+            if opening:
+                xps[j] = []
+            for hf in range(2):
+                if opening:
+                    if j == 0:
+                        xp = ps_xt.tile([P, HALF], F32, name="xp0", tag="xt")
+                    else:
+                        xp = ps_mm.tile([P, HALF], F32, name="xp", tag="mm")
+                    xps[j].append(xp)
+                    nc.tensor.matmul(
+                        out=xp[:], lhsT=ones_b[:], rhs=bo_pad[:, hf * HALF : (hf + 1) * HALF], start=True, stop=False
+                    )
+                xp = xps[j][hf]
+                for ci in sums:
+                    if ci == len(S_HEADS) - 1:
+                        nc.tensor.matmul(
+                            out=xp[:],
+                            lhsT=ident_b[:],
+                            rhs=a_raws[H][:, j, hf * HALF : (hf + 1) * HALF],
+                            start=False,
+                            stop=False,
+                        )
+                    for dd in range(4):
+                        nc.tensor.matmul(
+                            out=xp[:, dd * P : (dd + 1) * P],
+                            lhsT=accs[ci][:, hf * 4 + dd, j * P : (j + 1) * P],
+                            rhs=ident_f[:],
+                            is_transpose=True,
+                            start=False,
+                            stop=(ci == len(S_HEADS) - 1 and dd == 3),
+                        )
+
+        for n in range(-3, UNITS):
+            if in_range(n + 3):
+                pe_transposes(n + 3)
+                s_exits(n + 3)
+            if n == UNITS - 3:
+                pe_back(0, (0, 1))
+            if n == UNITS - 2:
+                pe_back(1, (0, 1))
+            if n == UNITS - 1:
+                pe_back(0, (2,))
+                pe_back(1, (2,))
+            if in_range(n):
+                pe_mm(n)
+            vector_empties = in_range(n) and n // 2 not in S_HEADS
+            if in_range(n + 2):
+                regroup(n + 2, s_copy if vector_empties else v_copy, 0, MAIN)
+                v_quant_a(n + 2)
+            if in_range(n + 1):
+                v_quant_w(n + 1)
+            if in_range(n + 2):
+                regroup(n + 2, g_copy if vector_empties else v_copy, MAIN, HALF)
+            if in_range(n):
+                take_out(n)
+            if (n + 7) % 2 == 0:
+                h = (n + 7) // 2
+                if 3 <= h < H:
+                    load_a(h, attn[:, h])
+                    load_w(h)
+                if h == H:
+                    load_a(H, query_inputs)
+                    nc.sync.dma_start(out=gamma_b[:], in_=gamma.partition_broadcast(P))
+                    nc.sync.dma_start(out=beta_b[:], in_=beta.partition_broadcast(P))
+
+        for j in range(4):
+            pe_back(j, (3,) if j < 2 else (0, 1, 2, 3))
+        for j in range(4):
+            stats = small.tile([P, 2, 6], F32, name="stats")
+            for hf in range(2):
+                nc.vector.bn_stats(out=stats[:, hf, :], in_=xps[j][hf][:])
+            mv = small.tile([P, 2], F32, name="mv")
+            nc.vector.bn_aggr(out=mv[:], in_=stats[:].rearrange("p a b -> p (a b)"))
+            ve = small.tile([P, 1], F32, name="ve")
+            nc.vector.tensor_scalar(out=ve[:], in0=mv[:, 1:2], scalar1=LN_EPS, scalar2=None, op0=ALU.add)
+            sd = small.tile([P, 1], F32, name="sd")
+            nc.scalar.activation(out=sd[:], in_=ve[:], func=ACT.Sqrt)
+            to = wgrp_pool.tile([P, 2, D], F32, name="to", tag="w_grp", align_bytes=64)
+            for hf in range(2):
+                nc.vector.scalar_tensor_tensor(
+                    out=to[:, 0, hf * HALF : (hf + 1) * HALF],
+                    in0=xps[j][hf][:],
+                    scalar=mv[:, 0:1],
+                    in1=gamma_b[:, hf * HALF : (hf + 1) * HALF],
+                    op0=ALU.subtract,
+                    op1=ALU.mult,
+                )
+            rstd = small.tile([P, 1], F32, name="rstd")
+            nc.vector.reciprocal(out=rstd[:], in_=sd[:])
+            if j == 3:
+                nc.vector.scalar_tensor_tensor(
+                    out=to[:, 1, :], in0=to[:, 0, :], scalar=rstd[:], in1=beta_b[:], op0=ALU.mult, op1=ALU.add
+                )
+            else:
+                nc.scalar.activation(out=to[:, 1, :], in_=to[:, 0, :], func=ACT.Copy, scale=rstd[:])
+                nc.gpsimd.tensor_tensor(out=to[:, 1, :], in0=to[:, 1, :], in1=beta_b[:], op=ALU.add)
+            nc.sync.dma_start(out=out[j // 2].rearrange("(p t) d -> p t d", t=2)[:, j % 2, :], in_=to[:, 1, :])

@@ -18,10 +18,11 @@ G = DV // 512
 DT = D // P
 HALF = D // 2
 UNITS = 2 * H
+LAST = UNITS - 1
 LN_EPS = 1e-3
 FLOPS = 2 * B * H * S * DV * D
 
-S_HEADS = (0, 2, 4, 7)
+S_HEADS = (0, 2, 4)
 MAIN = 384
 
 
@@ -37,9 +38,15 @@ def tile_multiheadattentionunit_pa_kernel(tc, attn, Wo, bo, query_inputs, gamma,
         agrp_pool = ctx.enter_context(tc.tile_pool(name="agrp", bufs=3))
         aq_pool = ctx.enter_context(tc.tile_pool(name="aq", bufs=3))
         small = ctx.enter_context(tc.tile_pool(name="small", bufs=4))
-        ps_xt = ctx.enter_context(tc.psum_pool(name="ps_xt", bufs=2))
-        ps_mm = ctx.enter_context(tc.psum_pool(name="ps_mm", bufs=6))
+        to_pool = ctx.enter_context(tc.tile_pool(name="to", bufs=4))
+        psum = ctx.enter_context(tc.psum_pool(name="psum", bufs=1))
         ctx.enter_context(tc.manual_schedule())
+
+        def bank(i, shape, dtype):
+            return psum.tile(shape, dtype, name="bank%d" % i)
+
+        def scalar_takes(n, dd):
+            return n // 2 in S_HEADS or (n // 2 == H - 1 and dd >= 2)
 
         a_raws = {}
         w_raws = {}
@@ -56,22 +63,26 @@ def tile_multiheadattentionunit_pa_kernel(tc, attn, Wo, bo, query_inputs, gamma,
             w_raw = wraw_pool.tile([P, 8 * D], BF16, name="w_raw")
             w_raws[h] = w_raw
             if h == 0:
-                rows = w_raw[:].rearrange("p (a e d) -> p a e d", a=2, e=4)
+                rows = w_raw[:].rearrange("p (x a e d) -> p x a e d", x=2, a=2, e=4)
                 for dh in range(2):
+                    if dh == 1:
+                        load_a(0, attn[:, 0])
                     for a in range(2):
                         nc.sync.dma_start(
-                            out=rows[:, a, :, dh * HALF : (dh + 1) * HALF],
+                            out=rows[:, dh, a, :, :],
                             in_=Wo[h, a * 512 : (a + 1) * 512, dh * HALF : (dh + 1) * HALF].rearrange(
                                 "(p e) d -> p e d", e=4
                             ),
                         )
             else:
-                nc.sync.dma_start(
-                    out=w_raw[:].rearrange("p (a x) -> p a x", a=2),
-                    in_=Wo[h].rearrange("(a p e) d -> p a (e d)", a=2, e=4),
-                )
+                for a in range(2):
+                    nc.sync.dma_start(
+                        out=w_raw[:, a * 4 * D : (a + 1) * 4 * D],
+                        in_=Wo[h, a * 512 : (a + 1) * 512].rearrange("(p e) d -> p (e d)", e=4),
+                    )
 
-        for h in range(3):
+        load_w(0)
+        for h in range(1, 3):
             load_a(h, attn[:, h])
             load_w(h)
 
@@ -89,27 +100,25 @@ def tile_multiheadattentionunit_pa_kernel(tc, attn, Wo, bo, query_inputs, gamma,
         nc.scalar.dma_start(out=bo_t[0 : H * DT, :], in_=bo.rearrange("h (t c) -> (h t) c", c=P))
         bo_pad = const.tile([P, D], BF16, name="bo_pad")
         nc.vector.memset(bo_pad[:], 0.0)
-        v_heads = [h for h in range(H) if h not in S_HEADS]
-        for r, h in enumerate(v_heads):
-            nc.scalar.dma_start(out=bo_pad[r : r + 1, :], in_=bo[h : h + 1, :])
+        for h in range(H - 1):
+            if not scalar_takes(2 * h, 0):
+                nc.scalar.dma_start(out=bo_pad[h : h + 1, :], in_=bo[h : h + 1, :])
+        for hf in range(2):
+            cols = slice(hf * HALF, hf * HALF + 2 * P)
+            nc.scalar.dma_start(out=bo_pad[H - 1 : H, cols], in_=bo[H - 1 : H, cols])
         gamma_b = const.tile([P, D], BF16, name="gamma_b")
         beta_b = const.tile([P, D], BF16, name="beta_b")
 
-        bT_ps = ps_xt.tile([P, P], BF16, name="bT_ps", tag="xt")
-        nc.tensor.transpose(bT_ps[:], bo_t[:], ident_b[:])
-        bpos = const.tile([P, P], F32, name="bpos")
-        nc.vector.tensor_copy(out=bpos[:], in_=bT_ps[:])
-        negb = const.tile([P, P], F32, name="negb")
-        nc.vector.tensor_scalar(out=negb[:], in0=bT_ps[:], scalar1=-1.0, scalar2=None, op0=ALU.mult)
-
         xts = {}
+        bpos = const.tile([P, P], F32, name="bpos")
+        negb = const.tile([P, P], F32, name="negb")
         a_grps = {}
         a_q = {}
         w_grps = {}
         w_lasts = {}
         w_q = {}
         pss = {}
-        accs = []
+        accs = [[[] for dd in range(4)] for hf in range(2)]
 
         def in_range(k):
             return 0 <= k < UNITS
@@ -119,7 +128,7 @@ def tile_multiheadattentionunit_pa_kernel(tc, attn, Wo, bo, query_inputs, gamma,
             a_raw = a_raws[h]
             xts[k] = []
             for half in range(2):
-                xt = ps_xt.tile([P, 2, 256], F32, name="xt", tag="xt")
+                xt = bank(6 + half, [P, 2, 256], F32)
                 for jj in range(2):
                     words = a_raw[:, 2 * half + jj, :].bitcast(F32)
                     for u in range(2):
@@ -173,11 +182,14 @@ def tile_multiheadattentionunit_pa_kernel(tc, attn, Wo, bo, query_inputs, gamma,
                 w_last_new = wlast_pool.tile([P, G * P * 4], BF16, name="w_last", align_bytes=64)
                 w_lasts[n] = w_last_new
                 dst = w_last_new[:].rearrange("p (g d t) -> p g d t", g=G, t=4)
-            rows = w_raws[h][:].rearrange("p (r d) -> p r d", r=8)
+            if h == 0:
+                rows = w_raws[h][:].rearrange("p (x r d) -> p x r d", x=2, r=8)[:, dh, :, :]
+            else:
+                rows = w_raws[h][:].rearrange("p (r d) -> p r d", r=8)[:, :, dh * HALF : (dh + 1) * HALF]
             for g in range(G):
                 copy(
                     dst[:, g, :, :].rearrange("p (c i) t -> p c t i", i=4),
-                    rows[:, 4 * g : 4 * g + 4, dh * HALF + c0 : dh * HALF + c1].rearrange("p t (c i) -> p c t i", i=4),
+                    rows[:, 4 * g : 4 * g + 4, c0:c1].rearrange("p t (c i) -> p c t i", i=4),
                 )
 
         def v_quant_w(n):
@@ -192,99 +204,96 @@ def tile_multiheadattentionunit_pa_kernel(tc, attn, Wo, bo, query_inputs, gamma,
                 )
             w_q[n] = (w_codes, w_sc)
 
-        def pe_mm(n):
-            h, dh = divmod(n, 2)
-            a_codes, a_sc = a_q[h]
+        def mm_group(n, dd, out_ps, c0, c1):
+            a_codes, a_sc = a_q[n // 2]
             w_codes, w_sc = w_q[n]
+            for g in range(G):
+                w0 = g * MAIN + dd * P if dd < 3 else 2 * MAIN + g * P
+                nc.tensor.matmul_mx(
+                    out=out_ps,
+                    lhsT=w_codes[:, w0 : w0 + P].bitcast(FP8X4),
+                    lhsT_scale=w_sc[:, w0 : w0 + P],
+                    rhs=a_codes[:, g * NS + c0 : g * NS + c1].bitcast(FP8X4),
+                    rhs_scale=a_sc[:, g * NS + c0 : g * NS + c1],
+                    start=(g == 0),
+                    stop=(g == G - 1),
+                )
+
+        def pe_mm(n):
             pss[n] = []
             for dd in range(4):
-                ps = ps_mm.tile([P, NS], F32, name="ps", tag="mm")
-                for g in range(G):
-                    w0 = g * MAIN + dd * P if dd < 3 else 2 * MAIN + g * P
-                    nc.tensor.matmul_mx(
-                        out=ps[:],
-                        lhsT=w_codes[:, w0 : w0 + P].bitcast(FP8X4),
-                        lhsT_scale=w_sc[:, w0 : w0 + P],
-                        rhs=a_codes[:, g * NS : (g + 1) * NS].bitcast(FP8X4),
-                        rhs_scale=a_sc[:, g * NS : (g + 1) * NS],
-                        start=(g == 0),
-                        stop=(g == G - 1),
-                    )
+                ps = bank((4 * n + dd) % 6 if n < LAST - 3 else dd, [P, NS], F32)
+                mm_group(n, dd, ps[:], 0, NS)
                 pss[n].append(ps)
 
-        def take_out(n):
-            h, dh = divmod(n, 2)
-            if h in S_HEADS and dh == 0:
-                acc_new = const.tile([P, DT, NS], F32, name="acc%d" % h)
-                accs.append(acc_new)
-            acc = accs[-1]
-            for dd in range(4):
-                dt = dh * 4 + dd
-                col = h * DT + dt
-                if h in S_HEADS:
-                    nc.scalar.activation(
-                        out=acc[:, dt, :], in_=pss[n][dd][:], func=ACT.Relu, bias=bpos[:, col : col + 1], scale=1.0
-                    )
-                else:
-                    nc.vector.scalar_tensor_tensor(
-                        out=acc[:, dt, :],
-                        in0=pss[n][dd][:],
-                        scalar=negb[:, col : col + 1],
-                        in1=acc[:, dt, :],
-                        op0=ALU.max,
-                        op1=ALU.add,
-                    )
+        def exit_sum(n, dd, src, c0, c1):
+            h, hf = divmod(n, 2)
+            col = h * DT + hf * 4 + dd
+            if scalar_takes(n, dd):
+                if c0 == 0:
+                    acc_new = const.tile([P, NS], F32, name="acc%d_%d" % (n, dd))
+                    accs[hf][dd].append(acc_new)
+                nc.scalar.activation(
+                    out=accs[hf][dd][-1][:, c0:c1], in_=src, func=ACT.Relu, bias=bpos[:, col : col + 1], scale=1.0
+                )
+            else:
+                acc = accs[hf][dd][-1]
+                nc.vector.scalar_tensor_tensor(
+                    out=acc[:, c0:c1],
+                    in0=src,
+                    scalar=negb[:, col : col + 1],
+                    in1=acc[:, c0:c1],
+                    op0=ALU.max,
+                    op1=ALU.add,
+                )
 
+        def take_out(n):
+            for dd in range(4):
+                exit_sum(n, dd, pss[n][dd][:], 0, NS)
+
+        X_BANKS = ((6, 7), (4, 5), (0, 1), (2, 3))
         xps = {}
 
-        def pe_back(j, sums):
-            opening = 0 in sums
-            if opening:
-                xps[j] = []
+        def x_open(j):
+            xps[j] = []
             for hf in range(2):
-                if opening:
-                    if j == 0:
-                        xp = ps_xt.tile([P, HALF], F32, name="xp0", tag="xt")
-                    else:
-                        xp = ps_mm.tile([P, HALF], F32, name="xp", tag="mm")
-                    xps[j].append(xp)
-                    nc.tensor.matmul(
-                        out=xp[:], lhsT=ones_b[:], rhs=bo_pad[:, hf * HALF : (hf + 1) * HALF], start=True, stop=False
-                    )
-                xp = xps[j][hf]
-                for ci in sums:
-                    if ci == len(S_HEADS) - 1:
-                        nc.tensor.matmul(
-                            out=xp[:],
-                            lhsT=ident_b[:],
-                            rhs=a_raws[H][:, j, hf * HALF : (hf + 1) * HALF],
-                            start=False,
-                            stop=False,
-                        )
-                    for dd in range(4):
-                        nc.tensor.matmul(
-                            out=xp[:, dd * P : (dd + 1) * P],
-                            lhsT=accs[ci][:, hf * 4 + dd, j * P : (j + 1) * P],
-                            rhs=ident_f[:],
-                            is_transpose=True,
-                            start=False,
-                            stop=(ci == len(S_HEADS) - 1 and dd == 3),
-                        )
+                xp = bank(X_BANKS[j][hf], [P, HALF], F32)
+                xps[j].append(xp)
+                cols = slice(hf * HALF, (hf + 1) * HALF)
+                nc.tensor.matmul(out=xp[:], lhsT=ones_b[:], rhs=bo_pad[:, cols], start=True, stop=False)
+                nc.tensor.matmul(out=xp[:], lhsT=ident_b[:], rhs=a_raws[H][:, j, cols], start=False, stop=False)
 
-        for n in range(-3, UNITS):
+        def x_add(j, hf, sums, stop=False):
+            for i, (dd, c) in enumerate(sums):
+                nc.tensor.matmul(
+                    out=xps[j][hf][:, dd * P : (dd + 1) * P],
+                    lhsT=accs[hf][dd][c][:, j * P : (j + 1) * P],
+                    rhs=ident_f[:],
+                    is_transpose=True,
+                    start=False,
+                    stop=stop and i == len(sums) - 1,
+                )
+
+        for n in range(-3, LAST):
             if in_range(n + 3):
                 pe_transposes(n + 3)
                 s_exits(n + 3)
-            if n == UNITS - 3:
-                pe_back(0, (0, 1))
-            if n == UNITS - 2:
-                pe_back(1, (0, 1))
-            if n == UNITS - 1:
-                pe_back(0, (2,))
-                pe_back(1, (2,))
+            if n == 0:
+                bT_ps = bank(7, [P, P], BF16)
+                nc.tensor.transpose(bT_ps[:], bo_t[:], ident_b[:])
+                nc.vector.tensor_copy(out=bpos[:], in_=bT_ps[:])
+                nc.vector.tensor_scalar(out=negb[:], in0=bT_ps[:], scalar1=-1.0, scalar2=None, op0=ALU.mult)
+            if n == LAST - 2:
+                x_open(0)
+                for hf in range(2):
+                    x_add(0, hf, [(dd, c) for dd in range(4) for c in range(2)])
+            if n == LAST - 1:
+                x_open(1)
+                for hf in range(2):
+                    x_add(1, hf, [(dd, c) for dd in range(4) for c in range(2)])
             if in_range(n):
                 pe_mm(n)
-            vector_empties = in_range(n) and n // 2 not in S_HEADS
+            vector_empties = in_range(n) and not scalar_takes(n, 0)
             if in_range(n + 2):
                 regroup(n + 2, s_copy if vector_empties else v_copy, 0, MAIN)
                 v_quant_a(n + 2)
@@ -304,35 +313,97 @@ def tile_multiheadattentionunit_pa_kernel(tc, attn, Wo, bo, query_inputs, gamma,
                     nc.sync.dma_start(out=gamma_b[:], in_=gamma.partition_broadcast(P))
                     nc.sync.dma_start(out=beta_b[:], in_=beta.partition_broadcast(P))
 
-        for j in range(4):
-            pe_back(j, (3,) if j < 2 else (0, 1, 2, 3))
-        for j in range(4):
-            stats = small.tile([P, 2, 6], F32, name="stats")
-            for hf in range(2):
-                nc.vector.bn_stats(out=stats[:, hf, :], in_=xps[j][hf][:])
+
+        stats = {}
+        shifts = {}
+        roots = {}
+        tos = {}
+
+        def last_batch(b):
+            for pair in range(2):
+                ps = bank(2 * b + pair, [P, 2, S], F32)
+                for e in range(2):
+                    mm_group(LAST, 2 * pair + e, ps[:, e, :], b * S, (b + 1) * S)
+                for e in range(2):
+                    exit_sum(LAST, 2 * pair + e, ps[:, e, :], b * S, (b + 1) * S)
+
+        def all_sums(hf):
+            return [(dd, c) for dd in range(4) for c in range(len(accs[hf][dd]))]
+
+        def v_stats(j, hf):
+            if hf == 0:
+                st = small.tile([P, 2, 6], F32, name="st")
+                stats[j] = st
+            nc.vector.bn_stats(out=stats[j][:, hf, :], in_=xps[j][hf][:])
+
+        def v_mean(j):
             mv = small.tile([P, 2], F32, name="mv")
-            nc.vector.bn_aggr(out=mv[:], in_=stats[:].rearrange("p a b -> p (a b)"))
-            ve = small.tile([P, 1], F32, name="ve")
-            nc.vector.tensor_scalar(out=ve[:], in0=mv[:, 1:2], scalar1=LN_EPS, scalar2=None, op0=ALU.add)
+            nc.vector.bn_aggr(out=mv[:], in_=stats[j][:].rearrange("p a b -> p (a b)"))
+            shifts[j] = (mv[:, 0:1], ALU.subtract)
+            s_root(j, mv[:, 1:2])
+
+        def s_root(j, var):
             sd = small.tile([P, 1], F32, name="sd")
-            nc.scalar.activation(out=sd[:], in_=ve[:], func=ACT.Sqrt)
-            to = wgrp_pool.tile([P, 2, D], F32, name="to", tag="w_grp", align_bytes=64)
+            nc.scalar.activation(out=sd[:], in_=var, func=ACT.Sqrt, bias=LN_EPS)
+            roots[j] = sd
+
+        def center(j):
+            to = to_pool.tile([P, 2, D], F32, name="to", align_bytes=64)
+            tos[j] = to
+            shift, op = shifts[j]
             for hf in range(2):
+                cols = slice(hf * HALF, (hf + 1) * HALF)
                 nc.vector.scalar_tensor_tensor(
-                    out=to[:, 0, hf * HALF : (hf + 1) * HALF],
-                    in0=xps[j][hf][:],
-                    scalar=mv[:, 0:1],
-                    in1=gamma_b[:, hf * HALF : (hf + 1) * HALF],
-                    op0=ALU.subtract,
-                    op1=ALU.mult,
+                    out=to[:, 0, cols], in0=xps[j][hf][:], scalar=shift, in1=gamma_b[:, cols], op0=op, op1=ALU.mult
                 )
+
+        def v_rstd(j):
             rstd = small.tile([P, 1], F32, name="rstd")
-            nc.vector.reciprocal(out=rstd[:], in_=sd[:])
-            if j == 3:
+            nc.vector.reciprocal(out=rstd[:], in_=roots[j][:])
+            roots[j] = rstd
+
+        def store(j, c0, c1):
+            dst = out[j // 2].rearrange("(p t) d -> p t d", t=2)[:, j % 2, c0:c1]
+            nc.sync.dma_start(out=dst, in_=tos[j][:, 1, c0:c1])
+
+        def finish_sg(j):
+            to = tos[j]
+            nc.scalar.activation(out=to[:, 1, :], in_=to[:, 0, :], func=ACT.Copy, scale=roots[j][:])
+            nc.gpsimd.tensor_tensor(out=to[:, 1, :], in0=to[:, 1, :], in1=beta_b[:], op=ALU.add)
+            store(j, 0, D)
+
+        def finish_v(j):
+            for hf in range(2):
+                cols = slice(hf * HALF, (hf + 1) * HALF)
                 nc.vector.scalar_tensor_tensor(
-                    out=to[:, 1, :], in0=to[:, 0, :], scalar=rstd[:], in1=beta_b[:], op0=ALU.mult, op1=ALU.add
+                    out=tos[j][:, 1, cols], in0=tos[j][:, 0, cols], scalar=roots[j][:], in1=beta_b[:, cols], op0=ALU.mult, op1=ALU.add
                 )
-            else:
-                nc.scalar.activation(out=to[:, 1, :], in_=to[:, 0, :], func=ACT.Copy, scale=rstd[:])
-                nc.gpsimd.tensor_tensor(out=to[:, 1, :], in0=to[:, 1, :], in1=beta_b[:], op=ALU.add)
-            nc.sync.dma_start(out=out[j // 2].rearrange("(p t) d -> p t d", t=2)[:, j % 2, :], in_=to[:, 1, :])
+                store(j, hf * HALF, (hf + 1) * HALF)
+
+        for j in range(2):
+            for hf in range(2):
+                x_add(j, hf, [(dd, 2) for dd in range(4) if scalar_takes(LAST, dd)])
+        last_batch(0)
+        late = [(dd, len(accs[1][dd]) - 1) for dd in range(4)]
+        for hf in range(2):
+            for j in range(2):
+                x_add(j, hf, late, True)
+                v_stats(j, hf)
+        for j in range(2):
+            v_mean(j)
+        last_batch(1)
+        for j in range(2):
+            center(j)
+            v_rstd(j)
+            finish_sg(j)
+        for j in range(2, 4):
+            x_open(j)
+            for hf in range(2):
+                x_add(j, hf, all_sums(hf), True)
+                v_stats(j, hf)
+            v_mean(j)
+            if j == 3:
+                finish_v(2)
+            center(j)
+            v_rstd(j)
+        finish_v(3)

@@ -59,9 +59,11 @@ def tile_multiheadattentionunit_pa_kernel(tc, attn, Wo, bo, query_inputs, gamma,
             )
             a_raws[h] = a_raw
 
-        def load_w(h):
-            w_raw = wraw_pool.tile([P, 8 * D], BF16, name="w_raw")
-            w_raws[h] = w_raw
+        def load_w(h, gs=range(G)):
+            if h not in w_raws:
+                w_raw_new = wraw_pool.tile([P, 8 * D], BF16, name="w_raw")
+                w_raws[h] = w_raw_new
+            w_raw = w_raws[h]
             if h == 0:
                 rows = w_raw[:].rearrange("p (x a e d) -> p x a e d", x=2, a=2, e=4)
                 for dh in range(2):
@@ -75,16 +77,18 @@ def tile_multiheadattentionunit_pa_kernel(tc, attn, Wo, bo, query_inputs, gamma,
                             ),
                         )
             else:
-                for a in range(2):
+                for a in gs:
                     nc.sync.dma_start(
                         out=w_raw[:, a * 4 * D : (a + 1) * 4 * D],
                         in_=Wo[h, a * 512 : (a + 1) * 512].rearrange("(p e) d -> p (e d)", e=4),
                     )
 
         load_w(0)
-        for h in range(1, 3):
-            load_a(h, attn[:, h])
-            load_w(h)
+        load_w(1, (0,))
+        load_a(1, attn[:, 1])
+        load_w(1, (1,))
+        load_a(2, attn[:, 2])
+        load_w(2)
 
         warm = const.tile([P, 1], F32, name="warm")
         nc.vector.memset(warm[:], 1.0)
@@ -169,7 +173,7 @@ def tile_multiheadattentionunit_pa_kernel(tc, attn, Wo, bo, query_inputs, gamma,
         def g_copy(o, i):
             nc.gpsimd.tensor_scalar(out=o, in0=i, scalar1=1.0, scalar2=0.0, op0=ALU.mult, op1=ALU.add)
 
-        def regroup(n, copy, c0, c1):
+        def regroup(n, copy, c0, c1, gs=range(G)):
             if c1 <= c0:
                 return
             h, dh = divmod(n, 2)
@@ -179,14 +183,15 @@ def tile_multiheadattentionunit_pa_kernel(tc, attn, Wo, bo, query_inputs, gamma,
                     w_grps[n] = w_grp_new
                 dst = w_grps[n][:].rearrange("p (g d t) -> p g d t", g=G, t=4)[:, :, c0:c1, :]
             else:
-                w_last_new = wlast_pool.tile([P, G * P * 4], BF16, name="w_last", align_bytes=64)
-                w_lasts[n] = w_last_new
-                dst = w_last_new[:].rearrange("p (g d t) -> p g d t", g=G, t=4)
+                if n not in w_lasts:
+                    w_last_new = wlast_pool.tile([P, G * P * 4], BF16, name="w_last", align_bytes=64)
+                    w_lasts[n] = w_last_new
+                dst = w_lasts[n][:].rearrange("p (g d t) -> p g d t", g=G, t=4)
             if h == 0:
                 rows = w_raws[h][:].rearrange("p (x r d) -> p x r d", x=2, r=8)[:, dh, :, :]
             else:
                 rows = w_raws[h][:].rearrange("p (r d) -> p r d", r=8)[:, :, dh * HALF : (dh + 1) * HALF]
-            for g in range(G):
+            for g in gs:
                 copy(
                     dst[:, g, :, :].rearrange("p (c i) t -> p c t i", i=4),
                     rows[:, 4 * g : 4 * g + 4, c0:c1].rearrange("p t (c i) -> p c t i", i=4),
@@ -274,15 +279,49 @@ def tile_multiheadattentionunit_pa_kernel(tc, attn, Wo, bo, query_inputs, gamma,
                     stop=stop and i == len(sums) - 1,
                 )
 
-        for n in range(-3, LAST):
+        regroup(0, v_copy, 0, MAIN)
+        regroup(0, v_copy, MAIN, HALF)
+        v_quant_w(0)
+        for k in range(2):
+            pe_transposes(k)
+            s_exits(k)
+        regroup(1, v_copy, 0, MAIN)
+        regroup(1, v_copy, MAIN, HALF)
+        load_a(3, attn[:, 3])
+        load_w(3)
+        v_quant_a(0)
+        v_quant_a(1)
+        bT_ps = bank(7, [P, P], BF16)
+        nc.tensor.transpose(bT_ps[:], bo_t[:], ident_b[:])
+        nc.vector.tensor_copy(out=bpos[:], in_=bT_ps[:])
+        nc.vector.tensor_scalar(out=negb[:], in0=bT_ps[:], scalar1=-1.0, scalar2=None, op0=ALU.mult)
+        v_quant_w(1)
+        pe_mm(0)
+        take_out(0)
+        regroup(2, v_copy, 0, MAIN, (0,))
+        for k in range(2, 4):
+            pe_transposes(k)
+            s_exits(k)
+        regroup(3, v_copy, 0, MAIN, (0,))
+        pe_mm(1)
+        take_out(1)
+        regroup(2, v_copy, 0, MAIN, (1,))
+        regroup(2, v_copy, MAIN, HALF)
+        v_quant_w(2)
+        v_quant_a(2)
+        v_quant_a(3)
+        regroup(3, v_copy, 0, MAIN, (1,))
+        regroup(3, v_copy, MAIN, HALF)
+        v_quant_w(3)
+        load_a(4, attn[:, 4])
+        load_w(4)
+        pe_transposes(4)
+        s_exits(4)
+
+        for n in range(2, LAST):
             if in_range(n + 3):
                 pe_transposes(n + 3)
                 s_exits(n + 3)
-            if n == 0:
-                bT_ps = bank(7, [P, P], BF16)
-                nc.tensor.transpose(bT_ps[:], bo_t[:], ident_b[:])
-                nc.vector.tensor_copy(out=bpos[:], in_=bT_ps[:])
-                nc.vector.tensor_scalar(out=negb[:], in0=bT_ps[:], scalar1=-1.0, scalar2=None, op0=ALU.mult)
             if n == LAST - 2:
                 x_open(0)
                 for hf in range(2):
@@ -297,7 +336,7 @@ def tile_multiheadattentionunit_pa_kernel(tc, attn, Wo, bo, query_inputs, gamma,
             if in_range(n + 2):
                 regroup(n + 2, s_copy if vector_empties else v_copy, 0, MAIN)
                 v_quant_a(n + 2)
-            if in_range(n + 1):
+            if n > 2:
                 v_quant_w(n + 1)
             if in_range(n + 2):
                 regroup(n + 2, g_copy if vector_empties else v_copy, MAIN, HALF)

@@ -83,7 +83,10 @@ def tile_multiheadattentionunit_pa_kernel(tc, attn, Wo, bo, query_inputs, gamma,
                         in_=Wo[h, a * 512 : (a + 1) * 512].rearrange("(p e) d -> p (e d)", e=4),
                     )
 
+        bo_t = const.tile([P, P], BF16, name="bo_t")
+        nc.vector.memset(bo_t[:], 0.0)
         load_w(0)
+        nc.sync.dma_start(out=bo_t[0 : H * DT, :], in_=bo.rearrange("h (t c) -> (h t) c", c=P))
         load_w(1, (0,))
         load_a(1, attn[:, 1])
         load_w(1, (1,))
@@ -99,17 +102,8 @@ def tile_multiheadattentionunit_pa_kernel(tc, attn, Wo, bo, query_inputs, gamma,
         make_identity(nc, ident_b[:])
         ones_b = const.tile([P, P], BF16, name="ones_b")
         nc.vector.memset(ones_b[:], 1.0)
-        bo_t = const.tile([P, P], BF16, name="bo_t")
-        nc.vector.memset(bo_t[:], 0.0)
-        nc.scalar.dma_start(out=bo_t[0 : H * DT, :], in_=bo.rearrange("h (t c) -> (h t) c", c=P))
         bo_pad = const.tile([P, D], BF16, name="bo_pad")
         nc.vector.memset(bo_pad[:], 0.0)
-        for h in range(H - 1):
-            if not scalar_takes(2 * h, 0):
-                nc.scalar.dma_start(out=bo_pad[h : h + 1, :], in_=bo[h : h + 1, :])
-        for hf in range(2):
-            cols = slice(hf * HALF, hf * HALF + 2 * P)
-            nc.scalar.dma_start(out=bo_pad[H - 1 : H, cols], in_=bo[H - 1 : H, cols])
         gamma_b = const.tile([P, D], BF16, name="gamma_b")
         beta_b = const.tile([P, D], BF16, name="beta_b")
 
@@ -347,6 +341,13 @@ def tile_multiheadattentionunit_pa_kernel(tc, attn, Wo, bo, query_inputs, gamma,
                 if 3 <= h < H:
                     load_a(h, attn[:, h])
                     load_w(h)
+                if h == H - 2:
+                    for hb in range(H - 1):
+                        if not scalar_takes(2 * hb, 0):
+                            nc.sync.dma_start(out=bo_pad[hb : hb + 1, :], in_=bo[hb : hb + 1, :])
+                    for hf in range(2):
+                        cols = slice(hf * HALF, hf * HALF + 2 * P)
+                        nc.sync.dma_start(out=bo_pad[H - 1 : H, cols], in_=bo[H - 1 : H, cols])
                 if h == H:
                     load_a(H, query_inputs)
                     nc.sync.dma_start(out=gamma_b[:], in_=gamma.partition_broadcast(P))

@@ -23,7 +23,7 @@ LN_EPS = 1e-3
 FLOPS = 2 * B * H * S * DV * D
 
 S_HEADS = (0, 2, 4)
-MAIN = 384
+MAIN = 352
 
 
 def tile_multiheadattentionunit_pa_kernel(tc, attn, Wo, bo, query_inputs, gamma, beta, out):
@@ -32,7 +32,6 @@ def tile_multiheadattentionunit_pa_kernel(tc, attn, Wo, bo, query_inputs, gamma,
         const = ctx.enter_context(tc.tile_pool(name="const", bufs=1))
         wraw_pool = ctx.enter_context(tc.tile_pool(name="wraw", bufs=3))
         wgrp_pool = ctx.enter_context(tc.tile_pool(name="wgrp", bufs=3))
-        wlast_pool = ctx.enter_context(tc.tile_pool(name="wlast", bufs=1))
         wq_pool = ctx.enter_context(tc.tile_pool(name="wq", bufs=4))
         araw_pool = ctx.enter_context(tc.tile_pool(name="araw", bufs=3))
         agrp_pool = ctx.enter_context(tc.tile_pool(name="agrp", bufs=3))
@@ -113,7 +112,6 @@ def tile_multiheadattentionunit_pa_kernel(tc, attn, Wo, bo, query_inputs, gamma,
         a_grps = {}
         a_q = {}
         w_grps = {}
-        w_lasts = {}
         w_q = {}
         pss = {}
         accs = [[[] for dd in range(4)] for hf in range(2)]
@@ -168,46 +166,32 @@ def tile_multiheadattentionunit_pa_kernel(tc, attn, Wo, bo, query_inputs, gamma,
             nc.gpsimd.tensor_scalar(out=o, in0=i, scalar1=1.0, scalar2=0.0, op0=ALU.mult, op1=ALU.add)
 
         def regroup(n, copy, c0, c1, gs=range(G)):
-            if c1 <= c0:
-                return
             h, dh = divmod(n, 2)
-            if c0 < MAIN:
-                if n not in w_grps:
-                    w_grp_new = wgrp_pool.tile([P, G * MAIN * 4], BF16, name="w_grp", tag="w_grp", align_bytes=64)
-                    w_grps[n] = w_grp_new
-                dst = w_grps[n][:].rearrange("p (g d t) -> p g d t", g=G, t=4)[:, :, c0:c1, :]
-            else:
-                if n not in w_lasts:
-                    w_last_new = wlast_pool.tile([P, G * P * 4], BF16, name="w_last", align_bytes=64)
-                    w_lasts[n] = w_last_new
-                dst = w_lasts[n][:].rearrange("p (g d t) -> p g d t", g=G, t=4)
+            if n not in w_grps:
+                w_grp_new = wgrp_pool.tile([P, G * HALF * 4], BF16, name="w_grp", align_bytes=64)
+                w_grps[n] = w_grp_new
+            dst = w_grps[n][:].rearrange("p (g d t) -> p g d t", g=G, t=4)
             if h == 0:
                 rows = w_raws[h][:].rearrange("p (x r d) -> p x r d", x=2, r=8)[:, dh, :, :]
             else:
                 rows = w_raws[h][:].rearrange("p (r d) -> p r d", r=8)[:, :, dh * HALF : (dh + 1) * HALF]
             for g in gs:
                 copy(
-                    dst[:, g, :, :].rearrange("p (c i) t -> p c t i", i=4),
+                    dst[:, g, c0:c1, :].rearrange("p (c i) t -> p c t i", i=4),
                     rows[:, 4 * g : 4 * g + 4, c0:c1].rearrange("p t (c i) -> p c t i", i=4),
                 )
 
         def v_quant_w(n):
             w_codes = wq_pool.tile([P, G * HALF], U32, name="w_codes", align_bytes=64)
             w_sc = wq_pool.tile([P, G * HALF], U8, name="w_sc", align_bytes=64)
-            for src, e0, e1, word0 in ((w_grps[n], 0, 2048, 0), (w_grps[n], 2048, 3072, 512), (w_lasts[n], 0, 1024, 768)):
-                words = (e1 - e0) // 4
-                nc.vector.quantize_mx(
-                    out=w_codes[:, word0 : word0 + words].bitcast(FP8X4),
-                    scales=w_sc[:, word0 : word0 + words],
-                    in_=src[:, e0:e1],
-                )
+            nc.vector.quantize_mx(out=w_codes[:].bitcast(FP8X4), scales=w_sc[:], in_=w_grps[n][:])
             w_q[n] = (w_codes, w_sc)
 
         def mm_group(n, dd, out_ps, c0, c1):
             a_codes, a_sc = a_q[n // 2]
             w_codes, w_sc = w_q[n]
             for g in range(G):
-                w0 = g * MAIN + dd * P if dd < 3 else 2 * MAIN + g * P
+                w0 = g * HALF + dd * P
                 nc.tensor.matmul_mx(
                     out=out_ps,
                     lhsT=w_codes[:, w0 : w0 + P].bitcast(FP8X4),
@@ -273,14 +257,12 @@ def tile_multiheadattentionunit_pa_kernel(tc, attn, Wo, bo, query_inputs, gamma,
                     stop=stop and i == len(sums) - 1,
                 )
 
-        regroup(0, v_copy, 0, MAIN)
-        regroup(0, v_copy, MAIN, HALF)
+        regroup(0, v_copy, 0, HALF)
         v_quant_w(0)
         for k in range(2):
             pe_transposes(k)
             s_exits(k)
-        regroup(1, v_copy, 0, MAIN)
-        regroup(1, v_copy, MAIN, HALF)
+        regroup(1, v_copy, 0, HALF)
         load_a(3, attn[:, 3])
         load_w(3)
         v_quant_a(0)
@@ -292,20 +274,18 @@ def tile_multiheadattentionunit_pa_kernel(tc, attn, Wo, bo, query_inputs, gamma,
         v_quant_w(1)
         pe_mm(0)
         take_out(0)
-        regroup(2, v_copy, 0, MAIN, (0,))
+        regroup(2, v_copy, 0, HALF, (0,))
         for k in range(2, 4):
             pe_transposes(k)
             s_exits(k)
-        regroup(3, v_copy, 0, MAIN, (0,))
+        regroup(3, v_copy, 0, HALF, (0,))
         pe_mm(1)
         take_out(1)
-        regroup(2, v_copy, 0, MAIN, (1,))
-        regroup(2, v_copy, MAIN, HALF)
+        regroup(2, v_copy, 0, HALF, (1,))
         v_quant_w(2)
         v_quant_a(2)
         v_quant_a(3)
-        regroup(3, v_copy, 0, MAIN, (1,))
-        regroup(3, v_copy, MAIN, HALF)
+        regroup(3, v_copy, 0, HALF, (1,))
         v_quant_w(3)
         load_a(4, attn[:, 4])
         load_w(4)
@@ -328,12 +308,17 @@ def tile_multiheadattentionunit_pa_kernel(tc, attn, Wo, bo, query_inputs, gamma,
                 pe_mm(n)
             vector_empties = in_range(n) and not scalar_takes(n, 0)
             if in_range(n + 2):
-                regroup(n + 2, s_copy if vector_empties else v_copy, 0, MAIN)
+                if vector_empties:
+                    regroup(n + 2, s_copy, 0, MAIN)
+                else:
+                    regroup(n + 2, v_copy, 0, HALF)
                 v_quant_a(n + 2)
             if n > 2:
                 v_quant_w(n + 1)
-            if in_range(n + 2):
-                regroup(n + 2, g_copy if vector_empties else v_copy, MAIN, HALF)
+            if in_range(n + 2) and vector_empties:
+                start = MAIN * 4
+                nc.vector.memset(w_grps[n + 2][:, start : start + 16], 0.0)
+                regroup(n + 2, g_copy, MAIN, HALF)
             if in_range(n):
                 take_out(n)
             if (n + 7) % 2 == 0:
@@ -388,13 +373,13 @@ def tile_multiheadattentionunit_pa_kernel(tc, attn, Wo, bo, query_inputs, gamma,
             roots[j] = sd
 
         def center(j):
-            to = to_pool.tile([P, 2, D], F32, name="to", align_bytes=64)
+            to = to_pool.tile([P, D], F32, name="to", align_bytes=64)
             tos[j] = to
             shift, op = shifts[j]
             for hf in range(2):
                 cols = slice(hf * HALF, (hf + 1) * HALF)
                 nc.vector.scalar_tensor_tensor(
-                    out=to[:, 0, cols], in0=xps[j][hf][:], scalar=shift, in1=gamma_b[:, cols], op0=op, op1=ALU.mult
+                    out=to[:, cols], in0=xps[j][hf][:], scalar=shift, in1=gamma_b[:, cols], op0=op, op1=ALU.mult
                 )
 
         def v_rstd(j):
@@ -404,19 +389,19 @@ def tile_multiheadattentionunit_pa_kernel(tc, attn, Wo, bo, query_inputs, gamma,
 
         def store(j, c0, c1):
             dst = out[j // 2].rearrange("(p t) d -> p t d", t=2)[:, j % 2, c0:c1]
-            nc.sync.dma_start(out=dst, in_=tos[j][:, 1, c0:c1])
+            nc.sync.dma_start(out=dst, in_=tos[j][:, c0:c1])
 
         def finish_sg(j):
             to = tos[j]
-            nc.scalar.activation(out=to[:, 1, :], in_=to[:, 0, :], func=ACT.Copy, scale=roots[j][:])
-            nc.gpsimd.tensor_tensor(out=to[:, 1, :], in0=to[:, 1, :], in1=beta_b[:], op=ALU.add)
+            nc.scalar.activation(out=to[:], in_=to[:], func=ACT.Copy, scale=roots[j][:])
+            nc.gpsimd.tensor_tensor(out=to[:], in0=to[:], in1=beta_b[:], op=ALU.add)
             store(j, 0, D)
 
         def finish_v(j):
             for hf in range(2):
                 cols = slice(hf * HALF, (hf + 1) * HALF)
                 nc.vector.scalar_tensor_tensor(
-                    out=tos[j][:, 1, cols], in0=tos[j][:, 0, cols], scalar=roots[j][:], in1=beta_b[:, cols], op0=ALU.mult, op1=ALU.add
+                    out=tos[j][:, cols], in0=tos[j][:, cols], scalar=roots[j][:], in1=beta_b[:, cols], op0=ALU.mult, op1=ALU.add
                 )
                 store(j, hf * HALF, (hf + 1) * HALF)
 

@@ -257,11 +257,20 @@ def tile_multiheadattentionunit_pa_kernel(tc, attn, Wo, bo, query_inputs, gamma,
                     stop=stop and i == len(sums) - 1,
                 )
 
+        def pe_keep_clock(times, h):
+            idle_ps = bank(5, [P, HALF], F32)
+            for i in range(times):
+                nc.tensor.matmul(
+                    out=idle_ps[:], lhsT=w_raws[h][:, 0:P], rhs=w_raws[h][:, 0:HALF], start=i == 0, stop=i == times - 1
+                )
+
         regroup(0, v_copy, 0, HALF)
         v_quant_w(0)
+        pe_keep_clock(6, 0)
         for k in range(2):
             pe_transposes(k)
             s_exits(k)
+            pe_keep_clock(2 + 2 * k, 0)
         regroup(1, v_copy, 0, HALF)
         load_a(3, attn[:, 3])
         load_w(3)
@@ -278,6 +287,8 @@ def tile_multiheadattentionunit_pa_kernel(tc, attn, Wo, bo, query_inputs, gamma,
         for k in range(2, 4):
             pe_transposes(k)
             s_exits(k)
+            if k == 2:
+                pe_keep_clock(2, 1)
         regroup(3, v_copy, 0, HALF, (0,))
         pe_mm(1)
         take_out(1)

from contextlib import ExitStack

import concourse.mybir as mybir
from concourse.masks import make_identity

F32 = mybir.dt.float32
BF16 = mybir.dt.bfloat16
U32 = mybir.dt.uint32
U8 = mybir.dt.uint8
FP8X4 = mybir.dt.float8_e4m3fn_x4
ALU = mybir.AluOpType
ACT = mybir.ActivationFunctionType

P = 128
B, H, S, DV, D = 2, 8, 256, 1024, 1024
NS = B * S
G = DV // 512
DT = D // P
HALF = D // 2
UNITS = 2 * H
LAST = UNITS - 1
LN_EPS = 1e-3
FLOPS = 2 * B * H * S * DV * D

S_HEADS = (0, 2, 4)
MAIN = 352


def tile_multiheadattentionunit_pa_kernel(tc, attn, Wo, bo, query_inputs, gamma, beta, out):
    nc = tc.nc
    with ExitStack() as ctx:
        const = ctx.enter_context(tc.tile_pool(name="const", bufs=1))
        wraw_pool = ctx.enter_context(tc.tile_pool(name="wraw", bufs=3))
        wgrp_pool = ctx.enter_context(tc.tile_pool(name="wgrp", bufs=3))
        wq_pool = ctx.enter_context(tc.tile_pool(name="wq", bufs=4))
        araw_pool = ctx.enter_context(tc.tile_pool(name="araw", bufs=3))
        agrp_pool = ctx.enter_context(tc.tile_pool(name="agrp", bufs=3))
        aq_pool = ctx.enter_context(tc.tile_pool(name="aq", bufs=3))
        small = ctx.enter_context(tc.tile_pool(name="small", bufs=4))
        to_pool = ctx.enter_context(tc.tile_pool(name="to", bufs=4))
        psum = ctx.enter_context(tc.psum_pool(name="psum", bufs=1))
        ctx.enter_context(tc.manual_schedule())

        def bank(i, shape, dtype):
            return psum.tile(shape, dtype, name="bank%d" % i)

        def scalar_takes(n, dd):
            return n // 2 in S_HEADS or (n // 2 == H - 1 and dd >= 2)

        a_raws = {}
        w_raws = {}

        def load_a(h, src):
            a_raw = araw_pool.tile([P, 4, DV], BF16, name="a_raw")
            nc.sync.dma_start(
                out=a_raw[:].rearrange("p (b t) k -> p b (t k)", b=B),
                in_=src.rearrange("b (p t) k -> p b (t k)", t=2),
            )
            a_raws[h] = a_raw

        def load_w(h, gs=range(G)):
            if h not in w_raws:
                w_raw_new = wraw_pool.tile([P, 8 * D], BF16, name="w_raw")
                w_raws[h] = w_raw_new
            w_raw = w_raws[h]
            if h == 0:
                rows = w_raw[:].rearrange("p (x a e d) -> p x a e d", x=2, a=2, e=4)
                for dh in range(2):
                    if dh == 1:
                        load_a(0, attn[:, 0])
                    for a in range(2):
                        nc.sync.dma_start(
                            out=rows[:, dh, a, :, :],
                            in_=Wo[h, a * 512 : (a + 1) * 512, dh * HALF : (dh + 1) * HALF].rearrange(
                                "(p e) d -> p e d", e=4
                            ),
                        )
            else:
                for a in gs:
                    nc.sync.dma_start(
                        out=w_raw[:, a * 4 * D : (a + 1) * 4 * D],
                        in_=Wo[h, a * 512 : (a + 1) * 512].rearrange("(p e) d -> p (e d)", e=4),
                    )

        bo_t = const.tile([P, P], BF16, name="bo_t")
        nc.vector.memset(bo_t[:], 0.0)
        load_w(0)
        nc.sync.dma_start(out=bo_t[0 : H * DT, :], in_=bo.rearrange("h (t c) -> (h t) c", c=P))
        load_w(1, (0,))
        load_a(1, attn[:, 1])
        load_w(1, (1,))
        load_a(2, attn[:, 2])
        load_w(2)

        warm = const.tile([P, 1], F32, name="warm")
        nc.vector.memset(warm[:], 1.0)
        nc.scalar.activation(out=warm[:], in_=warm[:], func=ACT.Sqrt)
        ident_f = const.tile([P, P], F32, name="ident_f")
        make_identity(nc, ident_f[:])
        ident_b = const.tile([P, P], BF16, name="ident_b")
        make_identity(nc, ident_b[:])
        ones_b = const.tile([P, P], BF16, name="ones_b")
        nc.vector.memset(ones_b[:], 1.0)
        bo_pad = const.tile([P, D], BF16, name="bo_pad")
        nc.vector.memset(bo_pad[:], 0.0)
        gamma_b = const.tile([P, D], BF16, name="gamma_b")
        beta_b = const.tile([P, D], BF16, name="beta_b")

        xts = {}
        bpos = const.tile([P, P], F32, name="bpos")
        negb = const.tile([P, P], F32, name="negb")
        a_grps = {}
        a_q = {}
        w_grps = {}
        w_q = {}
        pss = {}
        accs = [[[] for dd in range(4)] for hf in range(2)]

        def in_range(k):
            return 0 <= k < UNITS

        def pe_transposes(k):
            h, g = divmod(k, 2)
            a_raw = a_raws[h]
            xts[k] = []
            for half in range(2):
                xt = bank(6 + half, [P, 2, 256], F32)
                for jj in range(2):
                    words = a_raw[:, 2 * half + jj, :].bitcast(F32)
                    for u in range(2):
                        nc.tensor.transpose(
                            xt[:, u, jj * P : (jj + 1) * P], words[:, 256 * g + u : 256 * (g + 1) : 2], ident_f[:]
                        )
                xts[k].append(xt)

        def s_exits(k):
            a_grp = agrp_pool.tile([P, NS * 2], F32, name="a_grp", align_bytes=64)
            a_grp3 = a_grp[:].rearrange("p (c u) -> p c u", u=2)
            for half in range(2):
                nc.scalar.copy(
                    out=a_grp3[:, half * 256 : (half + 1) * 256, :],
                    in_=xts[k][half][:].rearrange("p u c -> p c u"),
                )
            a_grps[k] = a_grp

        def v_quant_a(k):
            h, g = divmod(k, 2)
            if g == 0:
                a_codes = aq_pool.tile([P, G * NS], U32, name="a_codes", align_bytes=64)
                a_sc = aq_pool.tile([P, G * NS], U8, name="a_sc", align_bytes=64)
                a_q[h] = (a_codes, a_sc)
            a_codes, a_sc = a_q[h]
            nc.vector.quantize_mx(
                out=a_codes[:, g * NS : (g + 1) * NS].bitcast(FP8X4),
                scales=a_sc[:, g * NS : (g + 1) * NS],
                in_=a_grps[k][:].bitcast(BF16),
            )

        def v_copy(o, i):
            nc.vector.tensor_copy(out=o, in_=i)

        def s_copy(o, i):
            nc.scalar.copy(out=o, in_=i)

        def g_copy(o, i):
            nc.gpsimd.tensor_scalar(out=o, in0=i, scalar1=1.0, scalar2=0.0, op0=ALU.mult, op1=ALU.add)

        def regroup(n, copy, c0, c1, gs=range(G)):
            h, dh = divmod(n, 2)
            if n not in w_grps:
                w_grp_new = wgrp_pool.tile([P, G * HALF * 4], BF16, name="w_grp", align_bytes=64)
                w_grps[n] = w_grp_new
            dst = w_grps[n][:].rearrange("p (g d t) -> p g d t", g=G, t=4)
            if h == 0:
                rows = w_raws[h][:].rearrange("p (x r d) -> p x r d", x=2, r=8)[:, dh, :, :]
            else:
                rows = w_raws[h][:].rearrange("p (r d) -> p r d", r=8)[:, :, dh * HALF : (dh + 1) * HALF]
            for g in gs:
                copy(
                    dst[:, g, c0:c1, :].rearrange("p (c i) t -> p c t i", i=4),
                    rows[:, 4 * g : 4 * g + 4, c0:c1].rearrange("p t (c i) -> p c t i", i=4),
                )

        def v_quant_w(n):
            w_codes = wq_pool.tile([P, G * HALF], U32, name="w_codes", align_bytes=64)
            w_sc = wq_pool.tile([P, G * HALF], U8, name="w_sc", align_bytes=64)
            nc.vector.quantize_mx(out=w_codes[:].bitcast(FP8X4), scales=w_sc[:], in_=w_grps[n][:])
            w_q[n] = (w_codes, w_sc)

        def mm_group(n, dd, out_ps, c0, c1):
            a_codes, a_sc = a_q[n // 2]
            w_codes, w_sc = w_q[n]
            for g in range(G):
                w0 = g * HALF + dd * P
                nc.tensor.matmul_mx(
                    out=out_ps,
                    lhsT=w_codes[:, w0 : w0 + P].bitcast(FP8X4),
                    lhsT_scale=w_sc[:, w0 : w0 + P],
                    rhs=a_codes[:, g * NS + c0 : g * NS + c1].bitcast(FP8X4),
                    rhs_scale=a_sc[:, g * NS + c0 : g * NS + c1],
                    start=(g == 0),
                    stop=(g == G - 1),
                )

        def pe_mm(n):
            pss[n] = []
            for dd in range(4):
                ps = bank((4 * n + dd) % 6 if n < LAST - 3 else dd, [P, NS], F32)
                mm_group(n, dd, ps[:], 0, NS)
                pss[n].append(ps)

        def exit_sum(n, dd, src, c0, c1):
            h, hf = divmod(n, 2)
            col = h * DT + hf * 4 + dd
            if scalar_takes(n, dd):
                if c0 == 0:
                    acc_new = const.tile([P, NS], F32, name="acc%d_%d" % (n, dd))
                    accs[hf][dd].append(acc_new)
                nc.scalar.activation(
                    out=accs[hf][dd][-1][:, c0:c1], in_=src, func=ACT.Relu, bias=bpos[:, col : col + 1], scale=1.0
                )
            else:
                acc = accs[hf][dd][-1]
                nc.vector.scalar_tensor_tensor(
                    out=acc[:, c0:c1],
                    in0=src,
                    scalar=negb[:, col : col + 1],
                    in1=acc[:, c0:c1],
                    op0=ALU.max,
                    op1=ALU.add,
                )

        def take_out(n):
            for dd in range(4):
                exit_sum(n, dd, pss[n][dd][:], 0, NS)

        X_BANKS = ((6, 7), (4, 5), (0, 1), (2, 3))
        xps = {}

        def x_open(j):
            xps[j] = []
            for hf in range(2):
                xp = bank(X_BANKS[j][hf], [P, HALF], F32)
                xps[j].append(xp)
                cols = slice(hf * HALF, (hf + 1) * HALF)
                nc.tensor.matmul(out=xp[:], lhsT=ones_b[:], rhs=bo_pad[:, cols], start=True, stop=False)
                nc.tensor.matmul(out=xp[:], lhsT=ident_b[:], rhs=a_raws[H][:, j, cols], start=False, stop=False)

        def x_add(j, hf, sums, stop=False):
            for i, (dd, c) in enumerate(sums):
                nc.tensor.matmul(
                    out=xps[j][hf][:, dd * P : (dd + 1) * P],
                    lhsT=accs[hf][dd][c][:, j * P : (j + 1) * P],
                    rhs=ident_f[:],
                    is_transpose=True,
                    start=False,
                    stop=stop and i == len(sums) - 1,
                )

        def pe_keep_clock(times, h):
            idle_ps = bank(5, [P, HALF], F32)
            for i in range(times):
                nc.tensor.matmul(
                    out=idle_ps[:], lhsT=w_raws[h][:, 0:P], rhs=w_raws[h][:, 0:HALF], start=i == 0, stop=i == times - 1
                )

        regroup(0, v_copy, 0, HALF)
        v_quant_w(0)
        pe_keep_clock(6, 0)
        for k in range(2):
            pe_transposes(k)
            s_exits(k)
            pe_keep_clock(2 + 2 * k, 0)
        regroup(1, v_copy, 0, HALF)
        load_a(3, attn[:, 3])
        load_w(3)
        v_quant_a(0)
        v_quant_a(1)
        bT_ps = bank(7, [P, P], BF16)
        nc.tensor.transpose(bT_ps[:], bo_t[:], ident_b[:])
        nc.vector.tensor_copy(out=bpos[:], in_=bT_ps[:])
        nc.vector.tensor_scalar(out=negb[:], in0=bT_ps[:], scalar1=-1.0, scalar2=None, op0=ALU.mult)
        v_quant_w(1)
        pe_mm(0)
        take_out(0)
        regroup(2, v_copy, 0, HALF, (0,))
        for k in range(2, 4):
            pe_transposes(k)
            s_exits(k)
            if k == 2:
                pe_keep_clock(2, 1)
        regroup(3, v_copy, 0, HALF, (0,))
        pe_mm(1)
        take_out(1)
        regroup(2, v_copy, 0, HALF, (1,))
        v_quant_w(2)
        v_quant_a(2)
        v_quant_a(3)
        regroup(3, v_copy, 0, HALF, (1,))
        v_quant_w(3)
        load_a(4, attn[:, 4])
        load_w(4)
        pe_transposes(4)
        s_exits(4)

        for n in range(2, LAST):
            if in_range(n + 3):
                pe_transposes(n + 3)
                s_exits(n + 3)
            if n == LAST - 2:
                x_open(0)
                for hf in range(2):
                    x_add(0, hf, [(dd, c) for dd in range(4) for c in range(2)])
            if n == LAST - 1:
                x_open(1)
                for hf in range(2):
                    x_add(1, hf, [(dd, c) for dd in range(4) for c in range(2)])
            if in_range(n):
                pe_mm(n)
            vector_empties = in_range(n) and not scalar_takes(n, 0)
            if in_range(n + 2):
                if vector_empties:
                    regroup(n + 2, s_copy, 0, MAIN)
                else:
                    regroup(n + 2, v_copy, 0, HALF)
                v_quant_a(n + 2)
            if n > 2:
                v_quant_w(n + 1)
            if in_range(n + 2) and vector_empties:
                start = MAIN * 4
                nc.vector.memset(w_grps[n + 2][:, start : start + 16], 0.0)
                regroup(n + 2, g_copy, MAIN, HALF)
            if in_range(n):
                take_out(n)
            if (n + 7) % 2 == 0:
                h = (n + 7) // 2
                if 3 <= h < H:
                    load_a(h, attn[:, h])
                    load_w(h)
                if h == H - 2:
                    for hb in range(H - 1):
                        if not scalar_takes(2 * hb, 0):
                            nc.sync.dma_start(out=bo_pad[hb : hb + 1, :], in_=bo[hb : hb + 1, :])
                    for hf in range(2):
                        cols = slice(hf * HALF, hf * HALF + 2 * P)
                        nc.sync.dma_start(out=bo_pad[H - 1 : H, cols], in_=bo[H - 1 : H, cols])
                if h == H:
                    load_a(H, query_inputs)
                    nc.sync.dma_start(out=gamma_b[:], in_=gamma.partition_broadcast(P))
                    nc.sync.dma_start(out=beta_b[:], in_=beta.partition_broadcast(P))


        stats = {}
        shifts = {}
        roots = {}
        tos = {}

        def last_batch(b):
            for pair in range(2):
                ps = bank(2 * b + pair, [P, 2, S], F32)
                for e in range(2):
                    mm_group(LAST, 2 * pair + e, ps[:, e, :], b * S, (b + 1) * S)
                for e in range(2):
                    exit_sum(LAST, 2 * pair + e, ps[:, e, :], b * S, (b + 1) * S)

        def all_sums(hf):
            return [(dd, c) for dd in range(4) for c in range(len(accs[hf][dd]))]

        def v_stats(j, hf):
            if hf == 0:
                st = small.tile([P, 2, 6], F32, name="st")
                stats[j] = st
            nc.vector.bn_stats(out=stats[j][:, hf, :], in_=xps[j][hf][:])

        def v_mean(j):
            mv = small.tile([P, 2], F32, name="mv")
            nc.vector.bn_aggr(out=mv[:], in_=stats[j][:].rearrange("p a b -> p (a b)"))
            shifts[j] = (mv[:, 0:1], ALU.subtract)
            s_root(j, mv[:, 1:2])

        def s_root(j, var):
            sd = small.tile([P, 1], F32, name="sd")
            nc.scalar.activation(out=sd[:], in_=var, func=ACT.Sqrt, bias=LN_EPS)
            roots[j] = sd

        def center(j):
            to = to_pool.tile([P, D], F32, name="to", align_bytes=64)
            tos[j] = to
            shift, op = shifts[j]
            for hf in range(2):
                cols = slice(hf * HALF, (hf + 1) * HALF)
                nc.vector.scalar_tensor_tensor(
                    out=to[:, cols], in0=xps[j][hf][:], scalar=shift, in1=gamma_b[:, cols], op0=op, op1=ALU.mult
                )

        def v_rstd(j):
            rstd = small.tile([P, 1], F32, name="rstd")
            nc.vector.reciprocal(out=rstd[:], in_=roots[j][:])
            roots[j] = rstd

        def store(j, c0, c1):
            dst = out[j // 2].rearrange("(p t) d -> p t d", t=2)[:, j % 2, c0:c1]
            nc.sync.dma_start(out=dst, in_=tos[j][:, c0:c1])

        def finish_sg(j):
            to = tos[j]
            nc.scalar.activation(out=to[:], in_=to[:], func=ACT.Copy, scale=roots[j][:])
            nc.gpsimd.tensor_tensor(out=to[:], in0=to[:], in1=beta_b[:], op=ALU.add)
            store(j, 0, D)

        def finish_v(j):
            for hf in range(2):
                cols = slice(hf * HALF, (hf + 1) * HALF)
                nc.vector.scalar_tensor_tensor(
                    out=tos[j][:, cols], in0=tos[j][:, cols], scalar=roots[j][:], in1=beta_b[:, cols], op0=ALU.mult, op1=ALU.add
                )
                store(j, hf * HALF, (hf + 1) * HALF)

        for j in range(2):
            for hf in range(2):
                x_add(j, hf, [(dd, 2) for dd in range(4) if scalar_takes(LAST, dd)])
        last_batch(0)
        late = [(dd, len(accs[1][dd]) - 1) for dd in range(4)]
        for hf in range(2):
            for j in range(2):
                x_add(j, hf, late, True)
                v_stats(j, hf)
        for j in range(2):
            v_mean(j)
        last_batch(1)
        for j in range(2):
            center(j)
            v_rstd(j)
            finish_sg(j)
        for j in range(2, 4):
            x_open(j)
            for hf in range(2):
                x_add(j, hf, all_sums(hf), True)
                v_stats(j, hf)
            v_mean(j)
            if j == 3:
                finish_v(2)
            center(j)
            v_rstd(j)
        finish_v(3)
